import numpy as np
import ml_dtypes


def mxq(x, axis, fmt="e4m3"):
    dtype, down = {"e4m3": (ml_dtypes.float8_e4m3fn, 7), "e5m2": (ml_dtypes.float8_e5m2, 14)}[fmt]
    v = np.moveaxis(np.asarray(x, np.float32).astype(ml_dtypes.bfloat16).astype(np.float64), axis, -1)
    blocks = v.reshape(v.shape[:-1] + (-1, 32))
    amax = np.abs(blocks).max(-1, keepdims=True)
    byte = np.maximum(np.where(amax > 0, np.frexp(amax)[1] - 1 + 127, 0) - down, 1)
    scale = np.exp2(byte - 127.0)
    codes = (blocks / scale).astype(np.float32).astype(dtype).astype(np.float64)
    return np.moveaxis((codes * scale).reshape(v.shape), -1, axis)


WIDE = False


def mx_kscale(k):
    if not WIDE:
        return np.ones(k)
    levels = np.array([10, -10, 5, -5, 0])
    if k % 512:
        return np.exp2(np.random.permutation(np.resize(levels, k // 32))).repeat(32)
    a = np.empty((k // 512, 16))
    for p in range(k // 512):
        a[p, :8] = np.random.permutation(np.resize(levels, 8))
        for g in range(8):
            far = levels[np.abs(levels - a[p, g]) >= 10]
            a[p, g + 8] = far[np.random.randint(len(far))]
    return np.exp2(a.ravel()).repeat(32)


BF16 = ml_dtypes.bfloat16


def bf(x):
    return np.asarray(x, np.float32).astype(BF16)


def f64(x):
    return np.asarray(x).astype(np.float64)


N, IN_F, OUT_F = 4096, 512, 128
POW = 2


def draw0():
    s = mx_kscale(IN_F)
    u = np.exp2(np.round(np.log2(mx_kscale(N)) / 2))
    return {"input": bf(np.random.standard_normal((N, IN_F)) * s / (u * u)[:, None]),
            "adj": bf(np.random.uniform(0.0, 1.0, (N, N)) * 1.5 / N ** 0.25 * u),
            "weight": bf(np.random.uniform(-1.0, 1.0, (IN_F, OUT_F)) * 1.7 / np.sqrt(IN_F) / s[:, None]),
            "bias": bf(np.random.standard_normal(OUT_F) * 0.3)}


def core(input, adj, weight, bias):
    k_adj = f64(adj) ** POW
    support = mxq(f64(input), 1, "e4m3") @ mxq(f64(weight), 0, "e4m3")
    out = (mxq(k_adj, 1, "e4m3") @ mxq(support, 0, "e4m3")) + f64(bias)
    return np.where(out > 0, out, np.expm1(out))


def e4m3fn_bytes(y):
    return np.clip(np.asarray(y, np.float64), -448.0, 448.0).astype(np.float32).astype(ml_dtypes.float8_e4m3fn).view(np.uint8)


def e4m3fn_values(b):
    return np.asarray(b, np.uint8).view(ml_dtypes.float8_e4m3fn).astype(np.float64)


def setup_inputs():
    d = draw0()
    x0 = np.asarray(d['weight']).astype(np.float64)
    s = (np.max(np.abs(x0), axis=(1,), keepdims=True) / 448.0).astype(np.float32)
    out = {}
    for k, v in d.items():
        if k == 'weight':
            out['weight_bytes'] = e4m3fn_bytes(x0 / s.astype(np.float64))
            out['weight_scale'] = s
        else:
            out[k] = v
    return out


def reference(input, adj, weight_bytes, weight_scale, bias):
    return core(input, adj, e4m3fn_values(weight_bytes) * weight_scale.astype(np.float64), bias)

@@ -1,0 +1,297 @@
+from contextlib import ExitStack
+
+import concourse.mybir as mybir
+from concourse.masks import make_identity
+
+NODES, FEATS, OUTS = 4096, 512, 128
+FLOPS = 2 * NODES * FEATS * OUTS + 2 * NODES * NODES * OUTS
+
+F32 = mybir.dt.float32
+BF16 = mybir.dt.bfloat16
+U32 = mybir.dt.uint32
+U8 = mybir.dt.uint8
+FP8 = mybir.dt.float8_e4m3fn
+FP8X4 = mybir.dt.float8_e4m3fn_x4
+ALU = mybir.AluOpType
+ACT = mybir.ActivationFunctionType
+
+P = 128
+PASS = 512
+N_PASS = NODES // PASS
+N_CHUNK = NODES // PASS
+N_TILE = NODES // P
+V_PASSES = 6
+RAW_BUFS = 8
+ORDER_HEAD = ["x0", "x1", "x2", "x3", "a0", "x4", "x5", "a1", "x6", "x7"]
+
+
+def tile_netgraphconvolution_t_kernel(tc, inp, adj, weight_bytes, weight_scale, bias, out):
+    nc = tc.nc
+    with ExitStack() as ctx:
+        const = ctx.enter_context(tc.tile_pool(name="const", bufs=1))
+        pool = ctx.enter_context(tc.tile_pool(name="work", bufs=2))
+        psum = ctx.enter_context(tc.psum_pool(name="psum", bufs=2))
+
+        inp_v = inp.rearrange("(c p j) k -> c p j k", p=P, j=4)
+        adj_v = adj.rearrange("(g p j) k -> g j p k", p=P, j=4)
+        out_v = out.rearrange("(g p j) n -> g p j n", p=P, j=4)
+
+        jobs = [(name[0], int(name[1:])) for name in ORDER_HEAD]
+        jobs += [("a", i) for i in range(N_TILE) if ("a", i) not in jobs]
+
+        live = {}
+
+        def load(job):
+            kind, i = job
+            if kind == "x":
+                t = pool.tile([P, 4, FEATS], BF16, name="xraw", bufs=8, align_bytes=64)
+                nc.sync.dma_start(out=t[:], in_=inp_v[i])
+            else:
+                t = pool.tile([P, NODES], BF16, name="araw", bufs=RAW_BUFS, align_bytes=64)
+                nc.sync.dma_start(out=t[:], in_=adj_v[i // 4, i % 4])
+            live[("raw", job)] = t
+
+        ident = const.tile([P, P], F32, name="ident", align_bytes=64)
+        make_identity(nc, ident[:])
+        w_bytes = const.tile([P, 4, OUTS], U8, name="w_bytes", align_bytes=64)
+        w_scale = const.tile([P, 4], F32, name="w_scale", align_bytes=64)
+        w_grp = const.tile([P, OUTS, 4], BF16, name="w_grp", align_bytes=64)
+        w_codes = const.tile([P, OUTS], U32, name="w_codes", align_bytes=64)
+        w_sc = const.tile([P, OUTS], U8, name="w_sc", align_bytes=64)
+        b_row = const.tile([P, OUTS], BF16, name="b_row", align_bytes=64)
+        ones = const.tile([P, P], BF16, name="ones", align_bytes=64)
+        b_all = const.tile([P, 4, OUTS], F32, name="b_all", align_bytes=64)
+        warm = const.tile([P, 1], F32, name="warm", align_bytes=64)
+        s_codes = const.tile([P, N_PASS, OUTS], U32, name="s_codes", align_bytes=64)
+        s_sc = const.tile([P, N_PASS, OUTS], U8, name="s_sc", align_bytes=64)
+
+        with tc.manual_schedule():
+            nc.vector.memset(warm[:], 0.0)
+            nc.scalar.activation(out=warm[:], in_=warm[:], func=ACT.Exp)
+            nc.vector.memset(b_row[:], 0.0)
+            nc.vector.memset(ones[:], 1.0)
+            load(jobs[0])
+            nc.sync.dma_start(out=w_bytes[:], in_=weight_bytes.rearrange("(p t) n -> p t n", t=4))
+            nc.sync.dma_start(out=w_scale[:], in_=weight_scale.rearrange("(p t) o -> p (t o)", t=4))
+            load(jobs[1])
+            nc.sync.dma_start(out=b_row[0:1, :], in_=bias.rearrange("(o n) -> o n", o=1))
+            n_loaded = 2
+            while n_loaded < len(jobs) and not (jobs[n_loaded] == ("a", RAW_BUFS)):
+                load(jobs[n_loaded])
+                n_loaded += 1
+
+            for t in range(4):
+                nc.vector.tensor_scalar(
+                    out=w_grp[:, :, t], in0=w_bytes[:, t, :].bitcast(FP8),
+                    scalar1=w_scale[:, t : t + 1], scalar2=None, op0=ALU.mult,
+                )
+            nc.vector.quantize_mx(
+                out=w_codes[:].bitcast(FP8X4), scales=w_sc[:],
+                in_=w_grp[:].rearrange("p n t -> p (n t)"),
+            )
+
+            def square(job):
+                kind, i = job
+                if kind == "x":
+                    return
+                raw = live[("raw", job)]
+                sq = pool.tile([P, V_PASSES, 2, P, 2], BF16, name="sq", bufs=3, align_bytes=64)
+                src = raw[:, 0 : V_PASSES * PASS].rearrange("q (g p u e) -> q g u p e", p=P, u=2, e=2)
+                for u in (0, 1):
+                    nc.vector.tensor_tensor(
+                        out=sq[:, :, u], in0=src[:, :, u], in1=src[:, :, u], op=ALU.mult
+                    )
+                live[("sq", job)] = sq
+
+            def transposes(job):
+                kind, i = job
+                raw = live.pop(("raw", job))
+                banks = []
+                if kind == "x":
+                    words = raw[:].rearrange("p j k -> p (j k)").bitcast(F32)
+                    for h in range(2):
+                        bank = psum.tile([P, 2, 2, P], F32, name="tp", bufs=6)
+                        for jj in range(2):
+                            for u in range(2):
+                                base = (2 * h + jj) * 256
+                                nc.tensor.transpose(
+                                    bank[:, u, jj, :], words[:, base + u : base + 256 : 2], ident[:]
+                                )
+                        banks.append(bank)
+                else:
+                    sq = live.pop(("sq", job))
+                    sq_words = sq[:].rearrange("q g u p e -> q (g u p e)").bitcast(F32)
+                    words = raw[:].bitcast(F32)
+                    for h in range(4):
+                        bank = psum.tile([P, 2, 2, P], F32, name="tp", bufs=6)
+                        for gg in range(2):
+                            g = 2 * h + gg
+                            for u in range(2):
+                                if g < V_PASSES:
+                                    piece = sq_words[:, (2 * g + u) * P : (2 * g + u + 1) * P]
+                                else:
+                                    piece = words[:, 256 * g + u : 256 * (g + 1) : 2]
+                                nc.tensor.transpose(bank[:, u, gg, :], piece, ident[:])
+                        banks.append(bank)
+                live[("banks", job)] = banks
+
+            def copies(job):
+                kind, i = job
+                banks = live.pop(("banks", job))
+                if kind == "x":
+                    grp = pool.tile([P, 4 * PASS], BF16, name="xgrp", bufs=3, align_bytes=64)
+                else:
+                    grp = pool.tile([P, N_PASS * PASS], BF16, name="agrp", bufs=3, align_bytes=64)
+                for h, bank in enumerate(banks):
+                    dst = grp[:, 1024 * h : 1024 * (h + 1)]
+                    if kind == "a" and 2 * h >= V_PASSES:
+                        nc.scalar.activation(
+                            out=dst.rearrange("p (x u e) -> p x u e", u=2, e=2),
+                            in_=bank[:].bitcast(BF16).rearrange("p u g (r e) -> p (g r) u e", e=2),
+                            func=ACT.Square,
+                        )
+                    else:
+                        dst_w = dst.bitcast(F32).rearrange("p (x u) -> p x u", u=2)
+                        src_w = bank[:].rearrange("p u g r -> p (g r) u")
+                        if kind == "x" and h == 0:
+                            nc.vector.tensor_copy(out=dst_w, in_=src_w)
+                        else:
+                            nc.scalar.copy(out=dst_w, in_=src_w)
+                live[("grp", job)] = grp
+
+            def quantize(job):
+                kind, i = job
+                grp = live.pop(("grp", job))
+                width = PASS if kind == "x" else N_PASS * P
+                if kind == "x":
+                    codes = pool.tile([P, PASS], U32, name="xcodes", bufs=2, align_bytes=64)
+                    scales = pool.tile([P, PASS], U8, name="xscales", bufs=2, align_bytes=64)
+                else:
+                    codes = pool.tile([P, N_PASS * P], U32, name="acodes", bufs=6, align_bytes=64)
+                    scales = pool.tile([P, N_PASS * P], U8, name="ascales", bufs=6, align_bytes=64)
+                nc.vector.quantize_mx(out=codes[:].bitcast(FP8X4), scales=scales[:], in_=grp[:])
+                live[("codes", job)] = (codes, scales)
+
+            def support(c):
+                codes, scales = live.pop(("codes", ("x", c)))
+                acc = psum.tile([P, 4, OUTS], F32, name="acc", bufs=2)
+                for j in range(4):
+                    cols = slice(j * P, (j + 1) * P)
+                    nc.tensor.matmul_mx(
+                        out=acc[:, j, :], lhsT=codes[:, cols].bitcast(FP8X4), lhsT_scale=scales[:, cols],
+                        rhs=w_codes[:].bitcast(FP8X4), rhs_scale=w_sc[:], start=True, stop=True,
+                    )
+                grp = pool.tile([P, OUTS, 4], BF16, name="sgrp", bufs=2, align_bytes=64)
+                nc.scalar.copy(out=grp[:], in_=acc[:].rearrange("p j n -> p n j"))
+                live[("sgrp", c)] = grp
+
+            def support_quantize(c):
+                grp = live.pop(("sgrp", c))
+                nc.vector.quantize_mx(
+                    out=s_codes[:, c, :].bitcast(FP8X4), scales=s_sc[:, c, :],
+                    in_=grp[:].rearrange("p n t -> p (n t)"),
+                )
+
+            def group_of(i):
+                if i == N_TILE - 1:
+                    return i, 1
+                first = i - i % 4
+                return first, (3 if first == N_TILE - 4 else 4)
+
+            def aggregate(i):
+                codes, scales = live.pop(("codes", ("a", i)))
+                first, n = group_of(i)
+                if i == first:
+                    acc_new = psum.tile([P, 4, OUTS], F32, name="acc", bufs=2)
+                    live[("acc", first)] = acc_new
+                acc = live[("acc", first)]
+                for g in range(N_PASS):
+                    cols = slice(g * P, (g + 1) * P)
+                    nc.tensor.matmul_mx(
+                        out=acc[:, i - first, :], lhsT=codes[:, cols].bitcast(FP8X4), lhsT_scale=scales[:, cols],
+                        rhs=s_codes[:, g, :].bitcast(FP8X4), rhs_scale=s_sc[:, g, :],
+                        start=(g == 0), stop=(g == N_PASS - 1),
+                    )
+                return first if i == first + n - 1 else None
+
+            def flat(t, n):
+                return t[:, 0:n, :].rearrange("p j n -> p (j n)")
+
+            def finish_one(first):
+                n = group_of(first)[1]
+                acc = live.pop(("acc", first))
+                v = pool.tile([P, 4, OUTS], F32, name="v", bufs=2, align_bytes=64)
+                e = pool.tile([P, 4, OUTS], F32, name="e", bufs=2, align_bytes=64)
+                nc.vector.tensor_tensor(out=flat(v, n), in0=flat(acc, n), in1=flat(b_all, n), op=ALU.add)
+                nc.vector.tensor_scalar(out=flat(e, n), in0=flat(v, n), scalar1=0.0, scalar2=None, op0=ALU.min)
+                live[("fin", first)] = (v, e)
+
+            def finish_two(first):
+                v, e = live[("fin", first)]
+                n = group_of(first)[1]
+                nc.scalar.activation(out=flat(e, n), in_=flat(e, n), func=ACT.Exp)
+
+            def finish_three(first):
+                v, e = live.pop(("fin", first))
+                n = group_of(first)[1]
+                o = pool.tile([P, 4, OUTS], F32, name="o", bufs=3, align_bytes=64)
+                nc.vector.scalar_tensor_tensor(
+                    out=flat(o, n), in0=flat(e, n), scalar=1.0, in1=flat(v, n), op0=ALU.subtract, op1=ALU.max
+                )
+                j0 = first % 4
+                nc.sync.dma_start(out=out_v[first // 4][:, j0 : j0 + n, :], in_=o[:, 0:n, :])
+
+            bias_ps = psum.tile([P, 2, 2, P], F32, name="tp", bufs=6)
+            nc.tensor.matmul(bias_ps[:, 0, 0, :], lhsT=ones[:], rhs=b_row[:], start=True, stop=True)
+            for j in range(4):
+                nc.vector.tensor_copy(out=b_all[:, j, :], in_=bias_ps[:, 0, 0, :])
+
+            n_jobs = len(jobs)
+            square(jobs[0])
+            square(jobs[1])
+            transposes(jobs[0])
+            copies(jobs[0])
+            sup_todo = []
+            agg_todo = []
+            x_done = 0
+            fin1, fin2 = [], []
+            for s in range(n_jobs + 4):
+                ready = agg_todo
+                agg_todo = []
+                fin_new = []
+                sup_new = []
+                if 1 <= s <= n_jobs:
+                    ready.append(jobs[s - 1])
+                for job in ready:
+                    if job[0] == "x":
+                        support(job[1])
+                        sup_new.append(job[1])
+                    elif x_done < N_CHUNK:
+                        agg_todo.append(job)
+                    else:
+                        first = aggregate(job[1])
+                        if first is not None:
+                            fin_new.append(first)
+                for first in fin1:
+                    finish_two(first)
+                if s + 1 < n_jobs:
+                    nxt = jobs[s + 1]
+                    transposes(nxt)
+                    if nxt[0] == "a" and n_loaded < n_jobs:
+                        load(jobs[n_loaded])
+                        n_loaded += 1
+                if s + 2 < n_jobs:
+                    square(jobs[s + 2])
+                if s < n_jobs:
+                    quantize(jobs[s])
+                for c in sup_todo:
+                    support_quantize(c)
+                    x_done += 1
+                sup_todo = sup_new
+                if s + 1 < n_jobs:
+                    copies(jobs[s + 1])
+                for first in fin1:
+                    finish_three(first)
+                for first in fin_new:
+                    finish_one(first)
+                fin1 = fin_new

@@ -22,7 +22,13 @@ N_CHUNK = NODES // PASS
 N_TILE = NODES // P
 V_PASSES = 6
 RAW_BUFS = 8
-ORDER_HEAD = ["x0", "x1", "x2", "x3", "a0", "x4", "x5", "a1", "x6", "x7"]
+ORDER_HEAD = ["x0", "x1", "x2", "x3", "x4", "x5", "x6", "x7"]
+LEAD = 2
+LAG_Q = 2
+LAG_M = 3
+X_BANKS_ON_V = ()
+A_BANKS_ON_V = {30: (1,), 31: (0, 2)}
+MIN_ON_V = False
 
 
 def tile_netgraphconvolution_t_kernel(tc, inp, adj, weight_bytes, weight_scale, bias, out):
@@ -33,6 +39,7 @@ def tile_netgraphconvolution_t_kernel(tc, inp, adj, weight_bytes, weight_scale, 
         psum = ctx.enter_context(tc.psum_pool(name="psum", bufs=2))
 
         inp_v = inp.rearrange("(c p j) k -> c p j k", p=P, j=4)
+        inp_run = inp.rearrange("(c q u i e) k -> c u q i (e k)", q=16, u=2, i=8, e=2)
         adj_v = adj.rearrange("(g p j) k -> g j p k", p=P, j=4)
         out_v = out.rearrange("(g p j) n -> g p j n", p=P, j=4)
 
@@ -45,7 +52,11 @@ def tile_netgraphconvolution_t_kernel(tc, inp, adj, weight_bytes, weight_scale, 
             kind, i = job
             if kind == "x":
                 t = pool.tile([P, 4, FEATS], BF16, name="xraw", bufs=8, align_bytes=64)
-                nc.sync.dma_start(out=t[:], in_=inp_v[i])
+                if i < V_PASSES:
+                    for u in (0, 1):
+                        nc.sync.dma_start(out=t[:, 2 * u : 2 * u + 2, :], in_=inp_run[i, u])
+                else:
+                    nc.sync.dma_start(out=t[:], in_=inp_v[i])
             else:
                 t = pool.tile([P, NODES], BF16, name="araw", bufs=RAW_BUFS, align_bytes=64)
                 nc.sync.dma_start(out=t[:], in_=adj_v[i // 4, i % 4])
@@ -95,8 +106,8 @@ def tile_netgraphconvolution_t_kernel(tc, inp, adj, weight_bytes, weight_scale, 
                 if kind == "x":
                     return
                 raw = live[("raw", job)]
-                sq = pool.tile([P, V_PASSES, 2, P, 2], BF16, name="sq", bufs=3, align_bytes=64)
-                src = raw[:, 0 : V_PASSES * PASS].rearrange("q (g p u e) -> q g u p e", p=P, u=2, e=2)
+                sq = pool.tile([P, V_PASSES, 2, 16, 16], BF16, name="sq", bufs=3, align_bytes=64)
+                src = raw[:, 0 : V_PASSES * PASS].rearrange("q (g a u r) -> q g u a r", a=16, u=2, r=16)
                 for u in (0, 1):
                     nc.vector.tensor_tensor(
                         out=sq[:, :, u], in0=src[:, :, u], in1=src[:, :, u], op=ALU.mult
@@ -120,7 +131,7 @@ def tile_netgraphconvolution_t_kernel(tc, inp, adj, weight_bytes, weight_scale, 
                         banks.append(bank)
                 else:
                     sq = live.pop(("sq", job))
-                    sq_words = sq[:].rearrange("q g u p e -> q (g u p e)").bitcast(F32)
+                    sq_words = sq[:].rearrange("q g u a r -> q (g u a r)").bitcast(F32)
                     words = raw[:].bitcast(F32)
                     for h in range(4):
                         bank = psum.tile([P, 2, 2, P], F32, name="tp", bufs=6)
@@ -139,9 +150,9 @@ def tile_netgraphconvolution_t_kernel(tc, inp, adj, weight_bytes, weight_scale, 
                 kind, i = job
                 banks = live.pop(("banks", job))
                 if kind == "x":
-                    grp = pool.tile([P, 4 * PASS], BF16, name="xgrp", bufs=3, align_bytes=64)
+                    grp = pool.tile([P, 4 * PASS], BF16, name="xgrp", bufs=4, align_bytes=64)
                 else:
-                    grp = pool.tile([P, N_PASS * PASS], BF16, name="agrp", bufs=3, align_bytes=64)
+                    grp = pool.tile([P, N_PASS * PASS], BF16, name="agrp", bufs=4, align_bytes=64)
                 for h, bank in enumerate(banks):
                     dst = grp[:, 1024 * h : 1024 * (h + 1)]
                     if kind == "a" and 2 * h >= V_PASSES:
@@ -153,7 +164,7 @@ def tile_netgraphconvolution_t_kernel(tc, inp, adj, weight_bytes, weight_scale, 
                     else:
                         dst_w = dst.bitcast(F32).rearrange("p (x u) -> p x u", u=2)
                         src_w = bank[:].rearrange("p u g r -> p (g r) u")
-                        if kind == "x" and h == 0:
+                        if (kind == "x" and h in X_BANKS_ON_V) or (kind == "a" and h in A_BANKS_ON_V.get(i, ())):
                             nc.vector.tensor_copy(out=dst_w, in_=src_w)
                         else:
                             nc.scalar.copy(out=dst_w, in_=src_w)
@@ -223,13 +234,18 @@ def tile_netgraphconvolution_t_kernel(tc, inp, adj, weight_bytes, weight_scale, 
                 v = pool.tile([P, 4, OUTS], F32, name="v", bufs=2, align_bytes=64)
                 e = pool.tile([P, 4, OUTS], F32, name="e", bufs=2, align_bytes=64)
                 nc.vector.tensor_tensor(out=flat(v, n), in0=flat(acc, n), in1=flat(b_all, n), op=ALU.add)
-                nc.vector.tensor_scalar(out=flat(e, n), in0=flat(v, n), scalar1=0.0, scalar2=None, op0=ALU.min)
+                if MIN_ON_V or n < 4:
+                    nc.vector.tensor_scalar(out=flat(e, n), in0=flat(v, n), scalar1=0.0, scalar2=None, op0=ALU.min)
                 live[("fin", first)] = (v, e)
 
             def finish_two(first):
                 v, e = live[("fin", first)]
                 n = group_of(first)[1]
-                nc.scalar.activation(out=flat(e, n), in_=flat(e, n), func=ACT.Exp)
+                if MIN_ON_V or n < 4:
+                    nc.scalar.activation(out=flat(e, n), in_=flat(e, n), func=ACT.Exp)
+                else:
+                    nc.scalar.activation(out=flat(e, n), in_=flat(v, n), func=ACT.Relu, scale=-1.0)
+                    nc.scalar.activation(out=flat(e, n), in_=flat(e, n), func=ACT.Exp, scale=-1.0)
 
             def finish_three(first):
                 v, e = live.pop(("fin", first))
@@ -247,21 +263,19 @@ def tile_netgraphconvolution_t_kernel(tc, inp, adj, weight_bytes, weight_scale, 
                 nc.vector.tensor_copy(out=b_all[:, j, :], in_=bias_ps[:, 0, 0, :])
 
             n_jobs = len(jobs)
-            square(jobs[0])
-            square(jobs[1])
-            transposes(jobs[0])
-            copies(jobs[0])
+            for k in range(LEAD):
+                square(jobs[k])
             sup_todo = []
             agg_todo = []
             x_done = 0
-            fin1, fin2 = [], []
-            for s in range(n_jobs + 4):
-                ready = agg_todo
-                agg_todo = []
+            fin1 = []
+            for s in range(n_jobs + LAG_M + 2):
                 fin_new = []
                 sup_new = []
-                if 1 <= s <= n_jobs:
-                    ready.append(jobs[s - 1])
+                ready = agg_todo
+                agg_todo = []
+                if 0 <= s - LAG_M < n_jobs:
+                    ready.append(jobs[s - LAG_M])
                 for job in ready:
                     if job[0] == "x":
                         support(job[1])
@@ -274,22 +288,21 @@ def tile_netgraphconvolution_t_kernel(tc, inp, adj, weight_bytes, weight_scale, 
                             fin_new.append(first)
                 for first in fin1:
                     finish_two(first)
-                if s + 1 < n_jobs:
-                    nxt = jobs[s + 1]
-                    transposes(nxt)
-                    if nxt[0] == "a" and n_loaded < n_jobs:
+                if s < n_jobs:
+                    transposes(jobs[s])
+                    if jobs[s][0] == "a" and n_loaded < n_jobs:
                         load(jobs[n_loaded])
                         n_loaded += 1
-                if s + 2 < n_jobs:
-                    square(jobs[s + 2])
-                if s < n_jobs:
-                    quantize(jobs[s])
+                if s + LEAD < n_jobs:
+                    square(jobs[s + LEAD])
+                if 0 <= s - LAG_Q < n_jobs:
+                    quantize(jobs[s - LAG_Q])
                 for c in sup_todo:
                     support_quantize(c)
                     x_done += 1
                 sup_todo = sup_new
-                if s + 1 < n_jobs:
-                    copies(jobs[s + 1])
+                if s < n_jobs:
+                    copies(jobs[s])
                 for first in fin1:
                     finish_three(first)
                 for first in fin_new:

@@ -20,15 +20,27 @@ PASS = 512
 N_PASS = NODES // PASS
 N_CHUNK = NODES // PASS
 N_TILE = NODES // P
-V_PASSES = 6
 RAW_BUFS = 8
-ORDER_HEAD = ["x0", "x1", "x2", "x3", "x4", "x5", "x6", "x7"]
+FOUR = (0, 3, 7, 10, 14, 17, 21, 24)
+EIGHT = ()
+BIAS_STEP = 6
+X_SPLIT = 1
+HALVES = ()
+A_SPLIT = (0,1)
+HEAD_WARM = 8
+X_WARM = 1
+A_WARM = 1
+W_AT = 1
+W_STEP = 1
+TAIL = (3, 1)
+SQ_BUFS = 3
+ORDER_HEAD = ["x0", "x1", "x2", "a0", "x3", "x4", "x5", "x6", "x7"]
 LEAD = 2
 LAG_Q = 2
-LAG_M = 3
-X_BANKS_ON_V = ()
-A_BANKS_ON_V = {30: (1,), 31: (0, 2)}
-MIN_ON_V = False
+LAG_M = 4
+X_BANKS_ON_V = {0: (0,), 1: (), 2: (), 3: (0,), 4: (0,), 5: (0,), 6: (), 7: ()}
+A_BANKS_ON_V = {31: (0, 2)}
+MIN_ON_V = True
 
 
 def tile_netgraphconvolution_t_kernel(tc, inp, adj, weight_bytes, weight_scale, bias, out):
@@ -39,7 +51,6 @@ def tile_netgraphconvolution_t_kernel(tc, inp, adj, weight_bytes, weight_scale, 
         psum = ctx.enter_context(tc.psum_pool(name="psum", bufs=2))
 
         inp_v = inp.rearrange("(c p j) k -> c p j k", p=P, j=4)
-        inp_run = inp.rearrange("(c q u i e) k -> c u q i (e k)", q=16, u=2, i=8, e=2)
         adj_v = adj.rearrange("(g p j) k -> g j p k", p=P, j=4)
         out_v = out.rearrange("(g p j) n -> g p j n", p=P, j=4)
 
@@ -52,14 +63,19 @@ def tile_netgraphconvolution_t_kernel(tc, inp, adj, weight_bytes, weight_scale, 
             kind, i = job
             if kind == "x":
                 t = pool.tile([P, 4, FEATS], BF16, name="xraw", bufs=8, align_bytes=64)
-                if i < V_PASSES:
-                    for u in (0, 1):
-                        nc.sync.dma_start(out=t[:, 2 * u : 2 * u + 2, :], in_=inp_run[i, u])
+                if i < X_SPLIT:
+                    for h in (0, 1):
+                        nc.sync.dma_start(out=t[:, 2 * h : 2 * h + 2, :], in_=inp_v[i][:, 2 * h : 2 * h + 2, :])
                 else:
                     nc.sync.dma_start(out=t[:], in_=inp_v[i])
             else:
                 t = pool.tile([P, NODES], BF16, name="araw", bufs=RAW_BUFS, align_bytes=64)
-                nc.sync.dma_start(out=t[:], in_=adj_v[i // 4, i % 4])
+                rows = adj_v[i // 4, i % 4]
+                if i in A_SPLIT:
+                    nc.sync.dma_start(out=t[:, NODES // 2 :], in_=rows[:, NODES // 2 :])
+                    nc.sync.dma_start(out=t[:, : NODES // 2], in_=rows[:, : NODES // 2])
+                else:
+                    nc.sync.dma_start(out=t[:], in_=rows)
             live[("raw", job)] = t
 
         ident = const.tile([P, P], F32, name="ident", align_bytes=64)
@@ -81,37 +97,38 @@ def tile_netgraphconvolution_t_kernel(tc, inp, adj, weight_bytes, weight_scale, 
             nc.scalar.activation(out=warm[:], in_=warm[:], func=ACT.Exp)
             nc.vector.memset(b_row[:], 0.0)
             nc.vector.memset(ones[:], 1.0)
-            load(jobs[0])
-            nc.sync.dma_start(out=w_bytes[:], in_=weight_bytes.rearrange("(p t) n -> p t n", t=4))
-            nc.sync.dma_start(out=w_scale[:], in_=weight_scale.rearrange("(p t) o -> p (t o)", t=4))
-            load(jobs[1])
-            nc.sync.dma_start(out=b_row[0:1, :], in_=bias.rearrange("(o n) -> o n", o=1))
-            n_loaded = 2
+            n_loaded = 0
             while n_loaded < len(jobs) and not (jobs[n_loaded] == ("a", RAW_BUFS)):
+                if n_loaded == W_AT:
+                    nc.sync.dma_start(out=w_bytes[:], in_=weight_bytes.rearrange("(p t) n -> p t n", t=4))
+                    nc.sync.dma_start(out=w_scale[:], in_=weight_scale.rearrange("(p t) o -> p (t o)", t=4))
+                    nc.sync.dma_start(out=b_row[0:1, :], in_=bias.rearrange("(o n) -> o n", o=1))
                 load(jobs[n_loaded])
                 n_loaded += 1
 
-            for t in range(4):
-                nc.vector.tensor_scalar(
-                    out=w_grp[:, :, t], in0=w_bytes[:, t, :].bitcast(FP8),
-                    scalar1=w_scale[:, t : t + 1], scalar2=None, op0=ALU.mult,
+            def weight():
+                for t in range(4):
+                    nc.vector.tensor_scalar(
+                        out=w_grp[:, :, t], in0=w_bytes[:, t, :].bitcast(FP8),
+                        scalar1=w_scale[:, t : t + 1], scalar2=None, op0=ALU.mult,
+                    )
+                nc.vector.quantize_mx(
+                    out=w_codes[:].bitcast(FP8X4), scales=w_sc[:],
+                    in_=w_grp[:].rearrange("p n t -> p (n t)"),
                 )
-            nc.vector.quantize_mx(
-                out=w_codes[:].bitcast(FP8X4), scales=w_sc[:],
-                in_=w_grp[:].rearrange("p n t -> p (n t)"),
-            )
+
+            def v_passes(i):
+                return 4 if i in FOUR else 8 if i in EIGHT else 6
 
             def square(job):
                 kind, i = job
                 if kind == "x":
                     return
                 raw = live[("raw", job)]
-                sq = pool.tile([P, V_PASSES, 2, 16, 16], BF16, name="sq", bufs=3, align_bytes=64)
-                src = raw[:, 0 : V_PASSES * PASS].rearrange("q (g a u r) -> q g u a r", a=16, u=2, r=16)
-                for u in (0, 1):
-                    nc.vector.tensor_tensor(
-                        out=sq[:, :, u], in0=src[:, :, u], in1=src[:, :, u], op=ALU.mult
-                    )
+                np = v_passes(i)
+                sq = pool.tile([P, 2, np * P, 2], BF16, name="sq", bufs=SQ_BUFS, align_bytes=64)
+                src = raw[:, 0 : np * PASS].rearrange("q (w u e) -> q u w e", u=2, e=2)
+                nc.vector.tensor_tensor(out=sq[:], in0=src, in1=src, op=ALU.mult)
                 live[("sq", job)] = sq
 
             def transposes(job):
@@ -128,22 +145,23 @@ def tile_netgraphconvolution_t_kernel(tc, inp, adj, weight_bytes, weight_scale, 
                                 nc.tensor.transpose(
                                     bank[:, u, jj, :], words[:, base + u : base + 256 : 2], ident[:]
                                 )
-                        banks.append(bank)
+                        banks.append((h, bank))
                 else:
                     sq = live.pop(("sq", job))
-                    sq_words = sq[:].rearrange("q g u a r -> q (g u a r)").bitcast(F32)
+                    sq_words = sq[:].rearrange("q u w e -> q (u w e)").bitcast(F32)
                     words = raw[:].bitcast(F32)
-                    for h in range(4):
+                    for h in (3, 2, 1, 0) if i in A_SPLIT else (0, 1, 2, 3):
                         bank = psum.tile([P, 2, 2, P], F32, name="tp", bufs=6)
                         for gg in range(2):
                             g = 2 * h + gg
                             for u in range(2):
-                                if g < V_PASSES:
-                                    piece = sq_words[:, (2 * g + u) * P : (2 * g + u + 1) * P]
+                                if g < v_passes(i):
+                                    first_word = (u * v_passes(i) + g) * P
+                                    piece = sq_words[:, first_word : first_word + P]
                                 else:
                                     piece = words[:, 256 * g + u : 256 * (g + 1) : 2]
                                 nc.tensor.transpose(bank[:, u, gg, :], piece, ident[:])
-                        banks.append(bank)
+                        banks.append((h, bank))
                 live[("banks", job)] = banks
 
             def copies(job):
@@ -153,9 +171,9 @@ def tile_netgraphconvolution_t_kernel(tc, inp, adj, weight_bytes, weight_scale, 
                     grp = pool.tile([P, 4 * PASS], BF16, name="xgrp", bufs=4, align_bytes=64)
                 else:
                     grp = pool.tile([P, N_PASS * PASS], BF16, name="agrp", bufs=4, align_bytes=64)
-                for h, bank in enumerate(banks):
+                for h, bank in banks:
                     dst = grp[:, 1024 * h : 1024 * (h + 1)]
-                    if kind == "a" and 2 * h >= V_PASSES:
+                    if kind == "a" and 2 * h >= v_passes(i):
                         nc.scalar.activation(
                             out=dst.rearrange("p (x u e) -> p x u e", u=2, e=2),
                             in_=bank[:].bitcast(BF16).rearrange("p u g (r e) -> p (g r) u e", e=2),
@@ -164,7 +182,7 @@ def tile_netgraphconvolution_t_kernel(tc, inp, adj, weight_bytes, weight_scale, 
                     else:
                         dst_w = dst.bitcast(F32).rearrange("p (x u) -> p x u", u=2)
                         src_w = bank[:].rearrange("p u g r -> p (g r) u")
-                        if (kind == "x" and h in X_BANKS_ON_V) or (kind == "a" and h in A_BANKS_ON_V.get(i, ())):
+                        if (kind == "x" and h in X_BANKS_ON_V.get(i, ())) or (kind == "a" and h in A_BANKS_ON_V.get(i, ())):
                             nc.vector.tensor_copy(out=dst_w, in_=src_w)
                         else:
                             nc.scalar.copy(out=dst_w, in_=src_w)
@@ -180,12 +198,22 @@ def tile_netgraphconvolution_t_kernel(tc, inp, adj, weight_bytes, weight_scale, 
                 else:
                     codes = pool.tile([P, N_PASS * P], U32, name="acodes", bufs=6, align_bytes=64)
                     scales = pool.tile([P, N_PASS * P], U8, name="ascales", bufs=6, align_bytes=64)
-                nc.vector.quantize_mx(out=codes[:].bitcast(FP8X4), scales=scales[:], in_=grp[:])
+                parts = 2 if (kind == "a" and i in HALVES) else 1
+                for q in range(parts):
+                    c0, c1 = q * width // parts, (q + 1) * width // parts
+                    nc.vector.quantize_mx(
+                        out=codes[:, c0:c1].bitcast(FP8X4), scales=scales[:, c0:c1], in_=grp[:, 4 * c0 : 4 * c1]
+                    )
                 live[("codes", job)] = (codes, scales)
+
+            def keep_clock(acc_slice, n):
+                for rep in range(n):
+                    nc.tensor.matmul(acc_slice, lhsT=ident[:], rhs=ident[:], start=True, stop=True)
 
             def support(c):
                 codes, scales = live.pop(("codes", ("x", c)))
                 acc = psum.tile([P, 4, OUTS], F32, name="acc", bufs=2)
+                keep_clock(acc[:, 0, :], X_WARM)
                 for j in range(4):
                     cols = slice(j * P, (j + 1) * P)
                     nc.tensor.matmul_mx(
@@ -204,10 +232,10 @@ def tile_netgraphconvolution_t_kernel(tc, inp, adj, weight_bytes, weight_scale, 
                 )
 
             def group_of(i):
-                if i == N_TILE - 1:
-                    return i, 1
                 first = i - i % 4
-                return first, (3 if first == N_TILE - 4 else 4)
+                if first == N_TILE - 4:
+                    return (first, TAIL[0]) if i < first + TAIL[0] else (first + TAIL[0], TAIL[1])
+                return first, 4
 
             def aggregate(i):
                 codes, scales = live.pop(("codes", ("a", i)))
@@ -216,6 +244,7 @@ def tile_netgraphconvolution_t_kernel(tc, inp, adj, weight_bytes, weight_scale, 
                     acc_new = psum.tile([P, 4, OUTS], F32, name="acc", bufs=2)
                     live[("acc", first)] = acc_new
                 acc = live[("acc", first)]
+                keep_clock(acc[:, i - first, :], A_WARM)
                 for g in range(N_PASS):
                     cols = slice(g * P, (g + 1) * P)
                     nc.tensor.matmul_mx(
@@ -257,14 +286,20 @@ def tile_netgraphconvolution_t_kernel(tc, inp, adj, weight_bytes, weight_scale, 
                 j0 = first % 4
                 nc.sync.dma_start(out=out_v[first // 4][:, j0 : j0 + n, :], in_=o[:, 0:n, :])
 
-            bias_ps = psum.tile([P, 2, 2, P], F32, name="tp", bufs=6)
-            nc.tensor.matmul(bias_ps[:, 0, 0, :], lhsT=ones[:], rhs=b_row[:], start=True, stop=True)
-            for j in range(4):
-                nc.vector.tensor_copy(out=b_all[:, j, :], in_=bias_ps[:, 0, 0, :])
+
+            def spread_bias():
+                bias_ps = psum.tile([P, 2, 2, P], F32, name="tp", bufs=6)
+                for j in range(4):
+                    nc.tensor.matmul(bias_ps[:, j // 2, j % 2, :], lhsT=ones[:], rhs=b_row[:], start=True, stop=True)
+                nc.scalar.copy(out=b_all[:].rearrange("p j n -> p (j n)"), in_=bias_ps[:].rearrange("p u g r -> p (u g r)"))
 
             n_jobs = len(jobs)
+            warm_ps = psum.tile([P, 4, OUTS], F32, name="acc", bufs=2)
+            keep_clock(warm_ps[:, 0, :], HEAD_WARM)
             for k in range(LEAD):
                 square(jobs[k])
+            if W_STEP < 0:
+                weight()
             sup_todo = []
             agg_todo = []
             x_done = 0
@@ -288,11 +323,15 @@ def tile_netgraphconvolution_t_kernel(tc, inp, adj, weight_bytes, weight_scale, 
                             fin_new.append(first)
                 for first in fin1:
                     finish_two(first)
+                if s == BIAS_STEP:
+                    spread_bias()
                 if s < n_jobs:
                     transposes(jobs[s])
                     if jobs[s][0] == "a" and n_loaded < n_jobs:
                         load(jobs[n_loaded])
                         n_loaded += 1
+                if s == W_STEP:
+                    weight()
                 if s + LEAD < n_jobs:
                     square(jobs[s + LEAD])
                 if 0 <= s - LAG_Q < n_jobs:
@@ -303,8 +342,8 @@ def tile_netgraphconvolution_t_kernel(tc, inp, adj, weight_bytes, weight_scale, 
                 sup_todo = sup_new
                 if s < n_jobs:
                     copies(jobs[s])
-                for first in fin1:
-                    finish_three(first)
                 for first in fin_new:
                     finish_one(first)
+                for first in fin1:
+                    finish_three(first)
                 fin1 = fin_new

@@ -20,26 +20,32 @@ PASS = 512
 N_PASS = NODES // PASS
 N_CHUNK = NODES // PASS
 N_TILE = NODES // P
-RAW_BUFS = 8
-FOUR = (0, 3, 7, 10, 14, 17, 21, 24)
+RAW_BUFS = 7
+FOUR = (0, 5, 10, 15, 20, 25)
 EIGHT = ()
-BIAS_STEP = 6
+BIAS_STEP = -1
 X_SPLIT = 1
-HALVES = ()
+HALVES = (31,)
 A_SPLIT = (0,1)
 HEAD_WARM = 8
-X_WARM = 1
-A_WARM = 1
+X_WARM = 0
+A_WARM = 0
+Q_FIRST = True
+XRAW_BUFS = 8
+ACODES_BUFS = 6
+AGRP_BUFS = 4
+S_PAIR = 2
+PAIRED = False
 W_AT = 1
-W_STEP = 1
+W_STEP = -1
 TAIL = (3, 1)
-SQ_BUFS = 3
-ORDER_HEAD = ["x0", "x1", "x2", "a0", "x3", "x4", "x5", "x6", "x7"]
+SQ_BUFS = 4
+ORDER_HEAD = ["x0", "x1", "a0", "x2", "x3", "a1", "x4", "x5", "a2", "x6", "x7"]
 LEAD = 2
 LAG_Q = 2
-LAG_M = 4
+LAG_M = 3
 X_BANKS_ON_V = {0: (0,), 1: (), 2: (), 3: (0,), 4: (0,), 5: (0,), 6: (), 7: ()}
-A_BANKS_ON_V = {31: (0, 2)}
+A_BANKS_ON_V = {31: (0,)}
 MIN_ON_V = True
 
 
@@ -52,6 +58,7 @@ def tile_netgraphconvolution_t_kernel(tc, inp, adj, weight_bytes, weight_scale, 
 
         inp_v = inp.rearrange("(c p j) k -> c p j k", p=P, j=4)
         adj_v = adj.rearrange("(g p j) k -> g j p k", p=P, j=4)
+        out_b = out.rearrange("(b g p j) n -> b p g (j n)", g=2, p=P, j=4)
         out_v = out.rearrange("(g p j) n -> g p j n", p=P, j=4)
 
         jobs = [(name[0], int(name[1:])) for name in ORDER_HEAD]
@@ -62,7 +69,7 @@ def tile_netgraphconvolution_t_kernel(tc, inp, adj, weight_bytes, weight_scale, 
         def load(job):
             kind, i = job
             if kind == "x":
-                t = pool.tile([P, 4, FEATS], BF16, name="xraw", bufs=8, align_bytes=64)
+                t = pool.tile([P, 4, FEATS], BF16, name="xraw", bufs=XRAW_BUFS, align_bytes=64)
                 if i < X_SPLIT:
                     for h in (0, 1):
                         nc.sync.dma_start(out=t[:, 2 * h : 2 * h + 2, :], in_=inp_v[i][:, 2 * h : 2 * h + 2, :])
@@ -72,8 +79,8 @@ def tile_netgraphconvolution_t_kernel(tc, inp, adj, weight_bytes, weight_scale, 
                 t = pool.tile([P, NODES], BF16, name="araw", bufs=RAW_BUFS, align_bytes=64)
                 rows = adj_v[i // 4, i % 4]
                 if i in A_SPLIT:
-                    nc.sync.dma_start(out=t[:, NODES // 2 :], in_=rows[:, NODES // 2 :])
-                    nc.sync.dma_start(out=t[:, : NODES // 2], in_=rows[:, : NODES // 2])
+                    for h in range(4):
+                        nc.sync.dma_start(out=t[:, 1024 * h : 1024 * (h + 1)], in_=rows[:, 1024 * h : 1024 * (h + 1)])
                 else:
                     nc.sync.dma_start(out=t[:], in_=rows)
             live[("raw", job)] = t
@@ -98,8 +105,12 @@ def tile_netgraphconvolution_t_kernel(tc, inp, adj, weight_bytes, weight_scale, 
             nc.vector.memset(b_row[:], 0.0)
             nc.vector.memset(ones[:], 1.0)
             n_loaded = 0
+            if W_AT == 0:
+                nc.sync.dma_start(out=w_bytes[:], in_=weight_bytes.rearrange("(p t) n -> p t n", t=4))
+                nc.sync.dma_start(out=w_scale[:], in_=weight_scale.rearrange("(p t) o -> p (t o)", t=4))
+                nc.sync.dma_start(out=b_row[0:1, :], in_=bias.rearrange("(o n) -> o n", o=1))
             while n_loaded < len(jobs) and not (jobs[n_loaded] == ("a", RAW_BUFS)):
-                if n_loaded == W_AT:
+                if n_loaded == W_AT and W_AT > 0:
                     nc.sync.dma_start(out=w_bytes[:], in_=weight_bytes.rearrange("(p t) n -> p t n", t=4))
                     nc.sync.dma_start(out=w_scale[:], in_=weight_scale.rearrange("(p t) o -> p (t o)", t=4))
                     nc.sync.dma_start(out=b_row[0:1, :], in_=bias.rearrange("(o n) -> o n", o=1))
@@ -128,7 +139,14 @@ def tile_netgraphconvolution_t_kernel(tc, inp, adj, weight_bytes, weight_scale, 
                 np = v_passes(i)
                 sq = pool.tile([P, 2, np * P, 2], BF16, name="sq", bufs=SQ_BUFS, align_bytes=64)
                 src = raw[:, 0 : np * PASS].rearrange("q (w u e) -> q u w e", u=2, e=2)
-                nc.vector.tensor_tensor(out=sq[:], in0=src, in1=src, op=ALU.mult)
+                if i in A_SPLIT:
+                    for h in range(np // 2):
+                        w0, w1 = 256 * h, 256 * (h + 1)
+                        nc.vector.tensor_tensor(
+                            out=sq[:, :, w0:w1, :], in0=src[:, :, w0:w1, :], in1=src[:, :, w0:w1, :], op=ALU.mult
+                        )
+                else:
+                    nc.vector.tensor_tensor(out=sq[:], in0=src, in1=src, op=ALU.mult)
                 live[("sq", job)] = sq
 
             def transposes(job):
@@ -150,7 +168,7 @@ def tile_netgraphconvolution_t_kernel(tc, inp, adj, weight_bytes, weight_scale, 
                     sq = live.pop(("sq", job))
                     sq_words = sq[:].rearrange("q u w e -> q (u w e)").bitcast(F32)
                     words = raw[:].bitcast(F32)
-                    for h in (3, 2, 1, 0) if i in A_SPLIT else (0, 1, 2, 3):
+                    for h in range(4):
                         bank = psum.tile([P, 2, 2, P], F32, name="tp", bufs=6)
                         for gg in range(2):
                             g = 2 * h + gg
@@ -170,7 +188,7 @@ def tile_netgraphconvolution_t_kernel(tc, inp, adj, weight_bytes, weight_scale, 
                 if kind == "x":
                     grp = pool.tile([P, 4 * PASS], BF16, name="xgrp", bufs=4, align_bytes=64)
                 else:
-                    grp = pool.tile([P, N_PASS * PASS], BF16, name="agrp", bufs=4, align_bytes=64)
+                    grp = pool.tile([P, N_PASS * PASS], BF16, name="agrp", bufs=AGRP_BUFS, align_bytes=64)
                 for h, bank in banks:
                     dst = grp[:, 1024 * h : 1024 * (h + 1)]
                     if kind == "a" and 2 * h >= v_passes(i):
@@ -193,11 +211,11 @@ def tile_netgraphconvolution_t_kernel(tc, inp, adj, weight_bytes, weight_scale, 
                 grp = live.pop(("grp", job))
                 width = PASS if kind == "x" else N_PASS * P
                 if kind == "x":
-                    codes = pool.tile([P, PASS], U32, name="xcodes", bufs=2, align_bytes=64)
-                    scales = pool.tile([P, PASS], U8, name="xscales", bufs=2, align_bytes=64)
+                    codes = pool.tile([P, PASS], U32, name="xcodes", bufs=3, align_bytes=64)
+                    scales = pool.tile([P, PASS], U8, name="xscales", bufs=3, align_bytes=64)
                 else:
-                    codes = pool.tile([P, N_PASS * P], U32, name="acodes", bufs=6, align_bytes=64)
-                    scales = pool.tile([P, N_PASS * P], U8, name="ascales", bufs=6, align_bytes=64)
+                    codes = pool.tile([P, N_PASS * P], U32, name="acodes", bufs=ACODES_BUFS, align_bytes=64)
+                    scales = pool.tile([P, N_PASS * P], U8, name="ascales", bufs=ACODES_BUFS, align_bytes=64)
                 parts = 2 if (kind == "a" and i in HALVES) else 1
                 for q in range(parts):
                     c0, c1 = q * width // parts, (q + 1) * width // parts
@@ -220,16 +238,22 @@ def tile_netgraphconvolution_t_kernel(tc, inp, adj, weight_bytes, weight_scale, 
                         out=acc[:, j, :], lhsT=codes[:, cols].bitcast(FP8X4), lhsT_scale=scales[:, cols],
                         rhs=w_codes[:].bitcast(FP8X4), rhs_scale=w_sc[:], start=True, stop=True,
                     )
-                grp = pool.tile([P, OUTS, 4], BF16, name="sgrp", bufs=2, align_bytes=64)
-                nc.scalar.copy(out=grp[:], in_=acc[:].rearrange("p j n -> p n j"))
-                live[("sgrp", c)] = grp
+                if c % S_PAIR == 0:
+                    grp_new = pool.tile([P, S_PAIR, OUTS, 4], BF16, name="sgrp", bufs=2, align_bytes=64)
+                    live[("sgrp", c // S_PAIR)] = grp_new
+                nc.scalar.copy(out=live[("sgrp", c // S_PAIR)][:, c % S_PAIR], in_=acc[:].rearrange("p j n -> p n j"))
 
             def support_quantize(c):
-                grp = live.pop(("sgrp", c))
+                if c % S_PAIR != S_PAIR - 1:
+                    return 0
+                grp = live.pop(("sgrp", c // S_PAIR))
+                c0 = c + 1 - S_PAIR
                 nc.vector.quantize_mx(
-                    out=s_codes[:, c, :].bitcast(FP8X4), scales=s_sc[:, c, :],
-                    in_=grp[:].rearrange("p n t -> p (n t)"),
+                    out=s_codes[:, c0 : c + 1, :].rearrange("p c n -> p (c n)").bitcast(FP8X4),
+                    scales=s_sc[:, c0 : c + 1, :].rearrange("p c n -> p (c n)"),
+                    in_=grp[:].rearrange("p c n t -> p (c n t)"),
                 )
+                return S_PAIR
 
             def group_of(i):
                 first = i - i % 4
@@ -254,38 +278,60 @@ def tile_netgraphconvolution_t_kernel(tc, inp, adj, weight_bytes, weight_scale, 
                     )
                 return first if i == first + n - 1 else None
 
-            def flat(t, n):
-                return t[:, 0:n, :].rearrange("p j n -> p (j n)")
+            def batch_of(first):
+                n = group_of(first)[1]
+                if PAIRED and first < N_TILE - 8:
+                    return first - first % 8, 8
+                return first, n
 
             def finish_one(first):
                 n = group_of(first)[1]
                 acc = live.pop(("acc", first))
-                v = pool.tile([P, 4, OUTS], F32, name="v", bufs=2, align_bytes=64)
-                e = pool.tile([P, 4, OUTS], F32, name="e", bufs=2, align_bytes=64)
-                nc.vector.tensor_tensor(out=flat(v, n), in0=flat(acc, n), in1=flat(b_all, n), op=ALU.add)
-                if MIN_ON_V or n < 4:
-                    nc.vector.tensor_scalar(out=flat(e, n), in0=flat(v, n), scalar1=0.0, scalar2=None, op0=ALU.min)
-                live[("fin", first)] = (v, e)
-
-            def finish_two(first):
-                v, e = live[("fin", first)]
-                n = group_of(first)[1]
-                if MIN_ON_V or n < 4:
-                    nc.scalar.activation(out=flat(e, n), in_=flat(e, n), func=ACT.Exp)
-                else:
-                    nc.scalar.activation(out=flat(e, n), in_=flat(v, n), func=ACT.Relu, scale=-1.0)
-                    nc.scalar.activation(out=flat(e, n), in_=flat(e, n), func=ACT.Exp, scale=-1.0)
-
-            def finish_three(first):
-                v, e = live.pop(("fin", first))
-                n = group_of(first)[1]
-                o = pool.tile([P, 4, OUTS], F32, name="o", bufs=3, align_bytes=64)
-                nc.vector.scalar_tensor_tensor(
-                    out=flat(o, n), in0=flat(e, n), scalar=1.0, in1=flat(v, n), op0=ALU.subtract, op1=ALU.max
+                b0, bn = batch_of(first)
+                if first == b0:
+                    v_new = pool.tile([P, 8 * OUTS], F32, name="v", bufs=2, align_bytes=64)
+                    live[("v", b0)] = v_new
+                v = live[("v", b0)]
+                c0 = (first - b0) * OUTS
+                nc.vector.tensor_tensor(
+                    out=v[:, c0 : c0 + n * OUTS], in0=acc[:, 0:n, :].rearrange("p j n -> p (j n)"),
+                    in1=b_all[:, 0:n, :].rearrange("p j n -> p (j n)"), op=ALU.add,
                 )
-                j0 = first % 4
-                nc.sync.dma_start(out=out_v[first // 4][:, j0 : j0 + n, :], in_=o[:, 0:n, :])
+                if first + n < b0 + bn:
+                    return None
+                cols = bn * OUTS
+                e = pool.tile([P, 8 * OUTS], F32, name="e", bufs=2, align_bytes=64)
+                if MIN_ON_V or bn < 4:
+                    nc.vector.tensor_scalar(out=e[:, :cols], in0=v[:, :cols], scalar1=0.0, scalar2=None, op0=ALU.min)
+                live[("e", b0)] = e
+                return b0
 
+            def finish_two(b0):
+                cols = batch_of(b0)[1] * OUTS
+                v, e = live[("v", b0)], live[("e", b0)]
+                if MIN_ON_V or cols < 4 * OUTS:
+                    nc.scalar.activation(out=e[:, :cols], in_=e[:, :cols], func=ACT.Exp)
+                else:
+                    nc.scalar.activation(out=e[:, :cols], in_=v[:, :cols], func=ACT.Relu, scale=-1.0)
+                    nc.scalar.activation(out=e[:, :cols], in_=e[:, :cols], func=ACT.Exp, scale=-1.0)
+
+            def finish_three(b0):
+                bn = batch_of(b0)[1]
+                cols = bn * OUTS
+                v, e = live.pop(("v", b0)), live.pop(("e", b0))
+                o = pool.tile([P, 8 * OUTS], F32, name="o", bufs=2, align_bytes=64)
+                nc.vector.scalar_tensor_tensor(
+                    out=o[:, :cols], in0=e[:, :cols], scalar=1.0, in1=v[:, :cols], op0=ALU.subtract, op1=ALU.max
+                )
+                if bn == 8:
+                    nc.sync.dma_start(
+                        out=out_b[b0 // 8], in_=o[:].rearrange("p (g c) -> p g c", g=2)
+                    )
+                else:
+                    j0 = b0 % 4
+                    nc.sync.dma_start(
+                        out=out_v[b0 // 4][:, j0 : j0 + bn, :], in_=o[:, :cols].rearrange("p (j n) -> p j n", n=OUTS)
+                    )
 
             def spread_bias():
                 bias_ps = psum.tile([P, 2, 2, P], F32, name="tp", bufs=6)
@@ -296,9 +342,13 @@ def tile_netgraphconvolution_t_kernel(tc, inp, adj, weight_bytes, weight_scale, 
             n_jobs = len(jobs)
             warm_ps = psum.tile([P, 4, OUTS], F32, name="acc", bufs=2)
             keep_clock(warm_ps[:, 0, :], HEAD_WARM)
+            if BIAS_STEP < 0:
+                spread_bias()
+            if W_STEP < -1:
+                weight()
             for k in range(LEAD):
                 square(jobs[k])
-            if W_STEP < 0:
+            if W_STEP == -1:
                 weight()
             sup_todo = []
             agg_todo = []
@@ -332,18 +382,22 @@ def tile_netgraphconvolution_t_kernel(tc, inp, adj, weight_bytes, weight_scale, 
                         n_loaded += 1
                 if s == W_STEP:
                     weight()
-                if s + LEAD < n_jobs:
+                if s + LEAD < n_jobs and not Q_FIRST:
                     square(jobs[s + LEAD])
                 if 0 <= s - LAG_Q < n_jobs:
                     quantize(jobs[s - LAG_Q])
                 for c in sup_todo:
-                    support_quantize(c)
-                    x_done += 1
+                    x_done += support_quantize(c)
+                if s + LEAD < n_jobs and Q_FIRST:
+                    square(jobs[s + LEAD])
                 sup_todo = sup_new
                 if s < n_jobs:
                     copies(jobs[s])
+                fin2 = []
                 for first in fin_new:
-                    finish_one(first)
+                    batch = finish_one(first)
+                    if batch is not None:
+                        fin2.append(batch)
                 for first in fin1:
                     finish_three(first)
-                fin1 = fin_new
+                fin1 = fin2

@@ -21,7 +21,7 @@ N_PASS = NODES // PASS
 N_CHUNK = NODES // PASS
 N_TILE = NODES // P
 RAW_BUFS = 7
-FOUR = (0, 5, 10, 15, 20, 25)
+FOUR = tuple(range(1, 32, 3))
 EIGHT = ()
 BIAS_STEP = -1
 X_SPLIT = 1
@@ -35,7 +35,7 @@ XRAW_BUFS = 8
 ACODES_BUFS = 6
 AGRP_BUFS = 4
 S_PAIR = 2
-PAIRED = False
+PAIRED = True
 W_AT = 1
 W_STEP = -1
 TAIL = (3, 1)
@@ -44,8 +44,8 @@ ORDER_HEAD = ["x0", "x1", "a0", "x2", "x3", "a1", "x4", "x5", "a2", "x6", "x7"]
 LEAD = 2
 LAG_Q = 2
 LAG_M = 3
-X_BANKS_ON_V = {0: (0,), 1: (), 2: (), 3: (0,), 4: (0,), 5: (0,), 6: (), 7: ()}
-A_BANKS_ON_V = {31: (0,)}
+X_BANKS_ON_V = {2: (0, 1)}
+A_BANKS_ON_V = {31: (0, 2)}
 MIN_ON_V = True
 
 

from contextlib import ExitStack

import concourse.mybir as mybir
from concourse.masks import make_identity

NODES, FEATS, OUTS = 4096, 512, 128
FLOPS = 2 * NODES * FEATS * OUTS + 2 * NODES * NODES * OUTS

F32 = mybir.dt.float32
BF16 = mybir.dt.bfloat16
U32 = mybir.dt.uint32
U8 = mybir.dt.uint8
FP8 = mybir.dt.float8_e4m3fn
FP8X4 = mybir.dt.float8_e4m3fn_x4
ALU = mybir.AluOpType
ACT = mybir.ActivationFunctionType

P = 128
PASS = 512
N_PASS = NODES // PASS
N_CHUNK = NODES // PASS
N_TILE = NODES // P
RAW_BUFS = 7
FOUR = tuple(range(1, 32, 3))
EIGHT = ()
BIAS_STEP = -1
X_SPLIT = 1
HALVES = (31,)
A_SPLIT = (0,1)
HEAD_WARM = 8
X_WARM = 0
A_WARM = 0
Q_FIRST = True
XRAW_BUFS = 8
ACODES_BUFS = 6
AGRP_BUFS = 4
S_PAIR = 2
PAIRED = True
W_AT = 1
W_STEP = -1
TAIL = (3, 1)
SQ_BUFS = 4
ORDER_HEAD = ["x0", "x1", "a0", "x2", "x3", "a1", "x4", "x5", "a2", "x6", "x7"]
LEAD = 2
LAG_Q = 2
LAG_M = 3
X_BANKS_ON_V = {2: (0, 1)}
A_BANKS_ON_V = {31: (0, 2)}
MIN_ON_V = True


def tile_netgraphconvolution_t_kernel(tc, inp, adj, weight_bytes, weight_scale, bias, out):
    nc = tc.nc
    with ExitStack() as ctx:
        const = ctx.enter_context(tc.tile_pool(name="const", bufs=1))
        pool = ctx.enter_context(tc.tile_pool(name="work", bufs=2))
        psum = ctx.enter_context(tc.psum_pool(name="psum", bufs=2))

        inp_v = inp.rearrange("(c p j) k -> c p j k", p=P, j=4)
        adj_v = adj.rearrange("(g p j) k -> g j p k", p=P, j=4)
        out_b = out.rearrange("(b g p j) n -> b p g (j n)", g=2, p=P, j=4)
        out_v = out.rearrange("(g p j) n -> g p j n", p=P, j=4)

        jobs = [(name[0], int(name[1:])) for name in ORDER_HEAD]
        jobs += [("a", i) for i in range(N_TILE) if ("a", i) not in jobs]

        live = {}

        def load(job):
            kind, i = job
            if kind == "x":
                t = pool.tile([P, 4, FEATS], BF16, name="xraw", bufs=XRAW_BUFS, align_bytes=64)
                if i < X_SPLIT:
                    for h in (0, 1):
                        nc.sync.dma_start(out=t[:, 2 * h : 2 * h + 2, :], in_=inp_v[i][:, 2 * h : 2 * h + 2, :])
                else:
                    nc.sync.dma_start(out=t[:], in_=inp_v[i])
            else:
                t = pool.tile([P, NODES], BF16, name="araw", bufs=RAW_BUFS, align_bytes=64)
                rows = adj_v[i // 4, i % 4]
                if i in A_SPLIT:
                    for h in range(4):
                        nc.sync.dma_start(out=t[:, 1024 * h : 1024 * (h + 1)], in_=rows[:, 1024 * h : 1024 * (h + 1)])
                else:
                    nc.sync.dma_start(out=t[:], in_=rows)
            live[("raw", job)] = t

        ident = const.tile([P, P], F32, name="ident", align_bytes=64)
        make_identity(nc, ident[:])
        w_bytes = const.tile([P, 4, OUTS], U8, name="w_bytes", align_bytes=64)
        w_scale = const.tile([P, 4], F32, name="w_scale", align_bytes=64)
        w_grp = const.tile([P, OUTS, 4], BF16, name="w_grp", align_bytes=64)
        w_codes = const.tile([P, OUTS], U32, name="w_codes", align_bytes=64)
        w_sc = const.tile([P, OUTS], U8, name="w_sc", align_bytes=64)
        b_row = const.tile([P, OUTS], BF16, name="b_row", align_bytes=64)
        ones = const.tile([P, P], BF16, name="ones", align_bytes=64)
        b_all = const.tile([P, 4, OUTS], F32, name="b_all", align_bytes=64)
        warm = const.tile([P, 1], F32, name="warm", align_bytes=64)
        s_codes = const.tile([P, N_PASS, OUTS], U32, name="s_codes", align_bytes=64)
        s_sc = const.tile([P, N_PASS, OUTS], U8, name="s_sc", align_bytes=64)

        with tc.manual_schedule():
            nc.vector.memset(warm[:], 0.0)
            nc.scalar.activation(out=warm[:], in_=warm[:], func=ACT.Exp)
            nc.vector.memset(b_row[:], 0.0)
            nc.vector.memset(ones[:], 1.0)
            n_loaded = 0
            if W_AT == 0:
                nc.sync.dma_start(out=w_bytes[:], in_=weight_bytes.rearrange("(p t) n -> p t n", t=4))
                nc.sync.dma_start(out=w_scale[:], in_=weight_scale.rearrange("(p t) o -> p (t o)", t=4))
                nc.sync.dma_start(out=b_row[0:1, :], in_=bias.rearrange("(o n) -> o n", o=1))
            while n_loaded < len(jobs) and not (jobs[n_loaded] == ("a", RAW_BUFS)):
                if n_loaded == W_AT and W_AT > 0:
                    nc.sync.dma_start(out=w_bytes[:], in_=weight_bytes.rearrange("(p t) n -> p t n", t=4))
                    nc.sync.dma_start(out=w_scale[:], in_=weight_scale.rearrange("(p t) o -> p (t o)", t=4))
                    nc.sync.dma_start(out=b_row[0:1, :], in_=bias.rearrange("(o n) -> o n", o=1))
                load(jobs[n_loaded])
                n_loaded += 1

            def weight():
                for t in range(4):
                    nc.vector.tensor_scalar(
                        out=w_grp[:, :, t], in0=w_bytes[:, t, :].bitcast(FP8),
                        scalar1=w_scale[:, t : t + 1], scalar2=None, op0=ALU.mult,
                    )
                nc.vector.quantize_mx(
                    out=w_codes[:].bitcast(FP8X4), scales=w_sc[:],
                    in_=w_grp[:].rearrange("p n t -> p (n t)"),
                )

            def v_passes(i):
                return 4 if i in FOUR else 8 if i in EIGHT else 6

            def square(job):
                kind, i = job
                if kind == "x":
                    return
                raw = live[("raw", job)]
                np = v_passes(i)
                sq = pool.tile([P, 2, np * P, 2], BF16, name="sq", bufs=SQ_BUFS, align_bytes=64)
                src = raw[:, 0 : np * PASS].rearrange("q (w u e) -> q u w e", u=2, e=2)
                if i in A_SPLIT:
                    for h in range(np // 2):
                        w0, w1 = 256 * h, 256 * (h + 1)
                        nc.vector.tensor_tensor(
                            out=sq[:, :, w0:w1, :], in0=src[:, :, w0:w1, :], in1=src[:, :, w0:w1, :], op=ALU.mult
                        )
                else:
                    nc.vector.tensor_tensor(out=sq[:], in0=src, in1=src, op=ALU.mult)
                live[("sq", job)] = sq

            def transposes(job):
                kind, i = job
                raw = live.pop(("raw", job))
                banks = []
                if kind == "x":
                    words = raw[:].rearrange("p j k -> p (j k)").bitcast(F32)
                    for h in range(2):
                        bank = psum.tile([P, 2, 2, P], F32, name="tp", bufs=6)
                        for jj in range(2):
                            for u in range(2):
                                base = (2 * h + jj) * 256
                                nc.tensor.transpose(
                                    bank[:, u, jj, :], words[:, base + u : base + 256 : 2], ident[:]
                                )
                        banks.append((h, bank))
                else:
                    sq = live.pop(("sq", job))
                    sq_words = sq[:].rearrange("q u w e -> q (u w e)").bitcast(F32)
                    words = raw[:].bitcast(F32)
                    for h in range(4):
                        bank = psum.tile([P, 2, 2, P], F32, name="tp", bufs=6)
                        for gg in range(2):
                            g = 2 * h + gg
                            for u in range(2):
                                if g < v_passes(i):
                                    first_word = (u * v_passes(i) + g) * P
                                    piece = sq_words[:, first_word : first_word + P]
                                else:
                                    piece = words[:, 256 * g + u : 256 * (g + 1) : 2]
                                nc.tensor.transpose(bank[:, u, gg, :], piece, ident[:])
                        banks.append((h, bank))
                live[("banks", job)] = banks

            def copies(job):
                kind, i = job
                banks = live.pop(("banks", job))
                if kind == "x":
                    grp = pool.tile([P, 4 * PASS], BF16, name="xgrp", bufs=4, align_bytes=64)
                else:
                    grp = pool.tile([P, N_PASS * PASS], BF16, name="agrp", bufs=AGRP_BUFS, align_bytes=64)
                for h, bank in banks:
                    dst = grp[:, 1024 * h : 1024 * (h + 1)]
                    if kind == "a" and 2 * h >= v_passes(i):
                        nc.scalar.activation(
                            out=dst.rearrange("p (x u e) -> p x u e", u=2, e=2),
                            in_=bank[:].bitcast(BF16).rearrange("p u g (r e) -> p (g r) u e", e=2),
                            func=ACT.Square,
                        )
                    else:
                        dst_w = dst.bitcast(F32).rearrange("p (x u) -> p x u", u=2)
                        src_w = bank[:].rearrange("p u g r -> p (g r) u")
                        if (kind == "x" and h in X_BANKS_ON_V.get(i, ())) or (kind == "a" and h in A_BANKS_ON_V.get(i, ())):
                            nc.vector.tensor_copy(out=dst_w, in_=src_w)
                        else:
                            nc.scalar.copy(out=dst_w, in_=src_w)
                live[("grp", job)] = grp

            def quantize(job):
                kind, i = job
                grp = live.pop(("grp", job))
                width = PASS if kind == "x" else N_PASS * P
                if kind == "x":
                    codes = pool.tile([P, PASS], U32, name="xcodes", bufs=3, align_bytes=64)
                    scales = pool.tile([P, PASS], U8, name="xscales", bufs=3, align_bytes=64)
                else:
                    codes = pool.tile([P, N_PASS * P], U32, name="acodes", bufs=ACODES_BUFS, align_bytes=64)
                    scales = pool.tile([P, N_PASS * P], U8, name="ascales", bufs=ACODES_BUFS, align_bytes=64)
                parts = 2 if (kind == "a" and i in HALVES) else 1
                for q in range(parts):
                    c0, c1 = q * width // parts, (q + 1) * width // parts
                    nc.vector.quantize_mx(
                        out=codes[:, c0:c1].bitcast(FP8X4), scales=scales[:, c0:c1], in_=grp[:, 4 * c0 : 4 * c1]
                    )
                live[("codes", job)] = (codes, scales)

            def keep_clock(acc_slice, n):
                for rep in range(n):
                    nc.tensor.matmul(acc_slice, lhsT=ident[:], rhs=ident[:], start=True, stop=True)

            def support(c):
                codes, scales = live.pop(("codes", ("x", c)))
                acc = psum.tile([P, 4, OUTS], F32, name="acc", bufs=2)
                keep_clock(acc[:, 0, :], X_WARM)
                for j in range(4):
                    cols = slice(j * P, (j + 1) * P)
                    nc.tensor.matmul_mx(
                        out=acc[:, j, :], lhsT=codes[:, cols].bitcast(FP8X4), lhsT_scale=scales[:, cols],
                        rhs=w_codes[:].bitcast(FP8X4), rhs_scale=w_sc[:], start=True, stop=True,
                    )
                if c % S_PAIR == 0:
                    grp_new = pool.tile([P, S_PAIR, OUTS, 4], BF16, name="sgrp", bufs=2, align_bytes=64)
                    live[("sgrp", c // S_PAIR)] = grp_new
                nc.scalar.copy(out=live[("sgrp", c // S_PAIR)][:, c % S_PAIR], in_=acc[:].rearrange("p j n -> p n j"))

            def support_quantize(c):
                if c % S_PAIR != S_PAIR - 1:
                    return 0
                grp = live.pop(("sgrp", c // S_PAIR))
                c0 = c + 1 - S_PAIR
                nc.vector.quantize_mx(
                    out=s_codes[:, c0 : c + 1, :].rearrange("p c n -> p (c n)").bitcast(FP8X4),
                    scales=s_sc[:, c0 : c + 1, :].rearrange("p c n -> p (c n)"),
                    in_=grp[:].rearrange("p c n t -> p (c n t)"),
                )
                return S_PAIR

            def group_of(i):
                first = i - i % 4
                if first == N_TILE - 4:
                    return (first, TAIL[0]) if i < first + TAIL[0] else (first + TAIL[0], TAIL[1])
                return first, 4

            def aggregate(i):
                codes, scales = live.pop(("codes", ("a", i)))
                first, n = group_of(i)
                if i == first:
                    acc_new = psum.tile([P, 4, OUTS], F32, name="acc", bufs=2)
                    live[("acc", first)] = acc_new
                acc = live[("acc", first)]
                keep_clock(acc[:, i - first, :], A_WARM)
                for g in range(N_PASS):
                    cols = slice(g * P, (g + 1) * P)
                    nc.tensor.matmul_mx(
                        out=acc[:, i - first, :], lhsT=codes[:, cols].bitcast(FP8X4), lhsT_scale=scales[:, cols],
                        rhs=s_codes[:, g, :].bitcast(FP8X4), rhs_scale=s_sc[:, g, :],
                        start=(g == 0), stop=(g == N_PASS - 1),
                    )
                return first if i == first + n - 1 else None

            def batch_of(first):
                n = group_of(first)[1]
                if PAIRED and first < N_TILE - 8:
                    return first - first % 8, 8
                return first, n

            def finish_one(first):
                n = group_of(first)[1]
                acc = live.pop(("acc", first))
                b0, bn = batch_of(first)
                if first == b0:
                    v_new = pool.tile([P, 8 * OUTS], F32, name="v", bufs=2, align_bytes=64)
                    live[("v", b0)] = v_new
                v = live[("v", b0)]
                c0 = (first - b0) * OUTS
                nc.vector.tensor_tensor(
                    out=v[:, c0 : c0 + n * OUTS], in0=acc[:, 0:n, :].rearrange("p j n -> p (j n)"),
                    in1=b_all[:, 0:n, :].rearrange("p j n -> p (j n)"), op=ALU.add,
                )
                if first + n < b0 + bn:
                    return None
                cols = bn * OUTS
                e = pool.tile([P, 8 * OUTS], F32, name="e", bufs=2, align_bytes=64)
                if MIN_ON_V or bn < 4:
                    nc.vector.tensor_scalar(out=e[:, :cols], in0=v[:, :cols], scalar1=0.0, scalar2=None, op0=ALU.min)
                live[("e", b0)] = e
                return b0

            def finish_two(b0):
                cols = batch_of(b0)[1] * OUTS
                v, e = live[("v", b0)], live[("e", b0)]
                if MIN_ON_V or cols < 4 * OUTS:
                    nc.scalar.activation(out=e[:, :cols], in_=e[:, :cols], func=ACT.Exp)
                else:
                    nc.scalar.activation(out=e[:, :cols], in_=v[:, :cols], func=ACT.Relu, scale=-1.0)
                    nc.scalar.activation(out=e[:, :cols], in_=e[:, :cols], func=ACT.Exp, scale=-1.0)

            def finish_three(b0):
                bn = batch_of(b0)[1]
                cols = bn * OUTS
                v, e = live.pop(("v", b0)), live.pop(("e", b0))
                o = pool.tile([P, 8 * OUTS], F32, name="o", bufs=2, align_bytes=64)
                nc.vector.scalar_tensor_tensor(
                    out=o[:, :cols], in0=e[:, :cols], scalar=1.0, in1=v[:, :cols], op0=ALU.subtract, op1=ALU.max
                )
                if bn == 8:
                    nc.sync.dma_start(
                        out=out_b[b0 // 8], in_=o[:].rearrange("p (g c) -> p g c", g=2)
                    )
                else:
                    j0 = b0 % 4
                    nc.sync.dma_start(
                        out=out_v[b0 // 4][:, j0 : j0 + bn, :], in_=o[:, :cols].rearrange("p (j n) -> p j n", n=OUTS)
                    )

            def spread_bias():
                bias_ps = psum.tile([P, 2, 2, P], F32, name="tp", bufs=6)
                for j in range(4):
                    nc.tensor.matmul(bias_ps[:, j // 2, j % 2, :], lhsT=ones[:], rhs=b_row[:], start=True, stop=True)
                nc.scalar.copy(out=b_all[:].rearrange("p j n -> p (j n)"), in_=bias_ps[:].rearrange("p u g r -> p (u g r)"))

            n_jobs = len(jobs)
            warm_ps = psum.tile([P, 4, OUTS], F32, name="acc", bufs=2)
            keep_clock(warm_ps[:, 0, :], HEAD_WARM)
            if BIAS_STEP < 0:
                spread_bias()
            if W_STEP < -1:
                weight()
            for k in range(LEAD):
                square(jobs[k])
            if W_STEP == -1:
                weight()
            sup_todo = []
            agg_todo = []
            x_done = 0
            fin1 = []
            for s in range(n_jobs + LAG_M + 2):
                fin_new = []
                sup_new = []
                ready = agg_todo
                agg_todo = []
                if 0 <= s - LAG_M < n_jobs:
                    ready.append(jobs[s - LAG_M])
                for job in ready:
                    if job[0] == "x":
                        support(job[1])
                        sup_new.append(job[1])
                    elif x_done < N_CHUNK:
                        agg_todo.append(job)
                    else:
                        first = aggregate(job[1])
                        if first is not None:
                            fin_new.append(first)
                for first in fin1:
                    finish_two(first)
                if s == BIAS_STEP:
                    spread_bias()
                if s < n_jobs:
                    transposes(jobs[s])
                    if jobs[s][0] == "a" and n_loaded < n_jobs:
                        load(jobs[n_loaded])
                        n_loaded += 1
                if s == W_STEP:
                    weight()
                if s + LEAD < n_jobs and not Q_FIRST:
                    square(jobs[s + LEAD])
                if 0 <= s - LAG_Q < n_jobs:
                    quantize(jobs[s - LAG_Q])
                for c in sup_todo:
                    x_done += support_quantize(c)
                if s + LEAD < n_jobs and Q_FIRST:
                    square(jobs[s + LEAD])
                sup_todo = sup_new
                if s < n_jobs:
                    copies(jobs[s])
                fin2 = []
                for first in fin_new:
                    batch = finish_one(first)
                    if batch is not None:
                        fin2.append(batch)
                for first in fin1:
                    finish_three(first)
                fin1 = fin2
